import numpy as np
import ml_dtypes


def mxq(x, axis, fmt="e4m3"):
    dtype, down = {"e4m3": (ml_dtypes.float8_e4m3fn, 7), "e5m2": (ml_dtypes.float8_e5m2, 14)}[fmt]
    v = np.moveaxis(np.asarray(x, np.float32).astype(ml_dtypes.bfloat16).astype(np.float64), axis, -1)
    blocks = v.reshape(v.shape[:-1] + (-1, 32))
    amax = np.abs(blocks).max(-1, keepdims=True)
    byte = np.maximum(np.where(amax > 0, np.frexp(amax)[1] - 1 + 127, 0) - down, 1)
    scale = np.exp2(byte - 127.0)
    codes = (blocks / scale).astype(np.float32).astype(dtype).astype(np.float64)
    return np.moveaxis((codes * scale).reshape(v.shape), -1, axis)


WIDE = False


def mx_kscale(k):
    if not WIDE:
        return np.ones(k)
    levels = np.array([10, -10, 5, -5, 0])
    if k % 512:
        return np.exp2(np.random.permutation(np.resize(levels, k // 32))).repeat(32)
    a = np.empty((k // 512, 16))
    for p in range(k // 512):
        a[p, :8] = np.random.permutation(np.resize(levels, 8))
        for g in range(8):
            far = levels[np.abs(levels - a[p, g]) >= 10]
            a[p, g + 8] = far[np.random.randint(len(far))]
    return np.exp2(a.ravel()).repeat(32)


BF16 = ml_dtypes.bfloat16


def bf(x):
    return np.asarray(x, np.float32).astype(BF16)


def f64(x):
    return np.asarray(x).astype(np.float64)


B, G, Z1, Z2, H, PD = 256, 16, 256, 256, 512, 512


def glin(x, W, b):
    y = mxq(x, 2, "e4m3").transpose(1, 0, 2) @ mxq(f64(W), 2, "e4m3").transpose(0, 2, 1)
    return y.transpose(1, 0, 2) + f64(b)


def setup_inputs():
    s = mx_kscale(H)
    h = np.maximum(np.random.standard_normal((B, G, H)), 0.0) + np.maximum(np.random.standard_normal((B, G, H)), 0.0)
    return {"h": bf(h * s),
            "W3": bf(np.random.standard_normal((G, H, H)) / np.sqrt(H) * s[None, :, None] / s[None, None, :]),
            "b3": bf(np.random.standard_normal((G, H)) * 0.2 * s),
            "Wo": bf(np.random.standard_normal((G, PD, H)) * 0.6 / np.sqrt(H) / s[None, None, :]),
            "bo": bf(np.random.standard_normal((G, PD)) * 0.2)}


def reference(h, W3, b3, Wo, bo):
    h = f64(h)
    h3 = np.maximum(glin(h, W3, b3), 0.0) + h
    out = glin(h3, Wo, bo)
    return out.reshape(B, G * PD)

@@ -1,0 +1,282 @@
+from contextlib import ExitStack
+
+import concourse.mybir as mybir
+from concourse.masks import make_identity
+
+F32 = mybir.dt.float32
+BF16 = mybir.dt.bfloat16
+U32 = mybir.dt.uint32
+U8 = mybir.dt.uint8
+FP8X4 = mybir.dt.float8_e4m3fn_x4
+ADD = mybir.AluOpType.add
+RELU = mybir.ActivationFunctionType.Relu
+
+P = 128
+B, G, H, PD = 256, 16, 512, 512
+FLOPS = 2 * B * G * H * (H + PD)
+
+W_BUFS = 8
+LOOKAHEAD = W_BUFS - 1
+HEAD_BIAS = {0: (1, 2, 3), 1: (4, 5, 6), 2: (7,)}
+H_CHUNKS = ((0, 2), (2, 4), (4, 8), (8, 12), (12, 16))
+
+
+def tile_linearwdecoder_pb_kernel(tc, h, W3, b3, Wo, bo, out):
+    nc = tc.nc
+    with ExitStack() as ctx:
+        const = ctx.enter_context(tc.tile_pool(name="const", bufs=1))
+        wnat = ctx.enter_context(tc.tile_pool(name="wnat", bufs=W_BUFS))
+        grp = ctx.enter_context(tc.tile_pool(name="grp", bufs=2))
+        cod = ctx.enter_context(tc.tile_pool(name="cod", bufs=2))
+        res = ctx.enter_context(tc.tile_pool(name="res", bufs=2))
+        tp = ctx.enter_context(tc.psum_pool(name="tp", bufs=4))
+        xp = ctx.enter_context(tc.psum_pool(name="xp", bufs=2))
+        yp = ctx.enter_context(tc.psum_pool(name="yp", bufs=2))
+        ctx.enter_context(tc.manual_schedule())
+
+        w3_view = W3.rearrange("g (q t) k -> q g (t k)", t=4)
+        wo_view = Wo.rearrange("g (q r) k -> q g (r k)", r=4)
+        h_view = h.rearrange("(bb m) g k -> m bb (g k)", m=P)
+        out_view = out.rearrange("(bb m) c -> m bb c", m=P)
+
+        b3n = const.tile([P, H], BF16)
+        bo16 = const.tile([P, PD], BF16)
+        nc.vector.memset(b3n[:], 0.0)
+        nc.vector.memset(bo16[:], 0.0)
+        nc.sync.dma_start(out=bo16[0:G, :], in_=bo)
+        nc.sync.dma_start(out=b3n[0:G, :], in_=b3)
+        ident = const.tile([P, P], F32)
+        make_identity(nc, ident[:])
+        identb = const.tile([P, P], BF16)
+        make_identity(nc, identb[:])
+        b3c = const.tile([P, 4 * G], F32)
+        bo_bc = const.tile([P, G * PD], BF16)
+
+        h_words = {}
+        w3n = {}
+        won = {}
+
+        def load_h(c):
+            g0, g1 = H_CHUNKS[c]
+            t = const.tile([P, 2 * (g1 - g0) * H], BF16, name="hnat%d" % c)
+            nc.sync.dma_start(
+                out=t[:].rearrange("p (bb x) -> p bb x", bb=2),
+                in_=h_view[:, :, g0 * H : g1 * H],
+            )
+            for g in range(g0, g1):
+                h_words[g] = (t, [(bb * (g1 - g0) + g - g0) * 256 + u for bb in range(2) for u in range(2)])
+
+        def load_w(g):
+            a = wnat.tile([P, 4 * H], BF16, tag="w3n", name="w3n")
+            nc.sync.dma_start(out=a[:], in_=w3_view[:, g])
+            w3n[g] = a
+            for c in range(len(H_CHUNKS)):
+                if H_CHUNKS[c][0] == g:
+                    load_h(c)
+            b = wnat.tile([P, 4 * H], BF16, tag="won", name="won")
+            nc.sync.dma_start(out=b[:], in_=wo_view[:, g])
+            won[g] = b
+
+        banks = {}
+        grouped = {}
+        w3c, woc, hc, h3c = {}, {}, {}, {}
+        h3g, xs, rs, ys, ots = {}, {}, {}, {}, {}
+
+        def flip(g, k):
+            if not 0 <= g < G:
+                return
+            if k < 2:
+                src, offsets = w3n[g], [512 * k + 256 * a + u for a in range(2) for u in range(2)]
+            elif k == 2:
+                src, offsets = h_words[g]
+            else:
+                src, offsets = won[g], [512 * (k - 3) + 256 * a + u for a in range(2) for u in range(2)]
+            bank = tp.tile([P, 512], F32, tag="tp", name="bank")
+            banks[(g, k)] = bank
+            words = src[:].bitcast(F32)
+            for i in range(4):
+                nc.tensor.transpose(
+                    bank[:, 128 * i : 128 * i + 128], words[:, offsets[i] : offsets[i] + 255 : 2], ident[:]
+                )
+
+        def copy_out(g, k):
+            if not 0 <= g < G:
+                return
+            if k == 0:
+                grouped[(g, "w3")] = grp.tile([P, 4 * H], BF16, tag="w3g", name="w3g", align_bytes=64)
+            if k == 2:
+                grouped[(g, "h")] = grp.tile([P, 4 * B], BF16, tag="hg", name="hg", align_bytes=64, bufs=3)
+            if k == 3:
+                grouped[(g, "wo")] = grp.tile([P, 4 * PD], BF16, tag="wog", name="wog", align_bytes=64)
+            if k < 2:
+                dst = grouped[(g, "w3")][:].bitcast(F32)[:, 512 * k : 512 * k + 512]
+            elif k == 2:
+                dst = grouped[(g, "h")][:].bitcast(F32)
+            else:
+                dst = grouped[(g, "wo")][:].bitcast(F32)[:, 512 * (k - 3) : 512 * (k - 3) + 512]
+            nc.scalar.copy(
+                out=dst.rearrange("p (a q u) -> p a q u", a=2, u=2),
+                in_=banks[(g, k)][:].rearrange("p (a u q) -> p a q u", a=2, u=2),
+            )
+
+        def bias3_to_partitions():
+            bank = tp.tile([P, 512], F32, tag="tp", name="b3bank")
+            words = b3n[:].bitcast(F32)
+            for u in range(2):
+                nc.tensor.transpose(bank[:, 128 * u : 128 * u + 128], words[:, u:256:2], ident[:])
+            nc.vector.tensor_copy(
+                out=b3c[:].rearrange("p (g u e) -> p u g e", u=2, e=2),
+                in_=bank[:, 0:256].bitcast(BF16).rearrange("p (u g e) -> p u g e", u=2, e=2)[:, :, 0:G, :],
+            )
+
+        def spread_bias(c):
+            bank = tp.tile([P, 1024], BF16, tag="tp", name="bbank")
+            for i in range(2):
+                g = 2 * c + i
+                nc.tensor.matmul(
+                    bank[:, 512 * i : 512 * i + 512],
+                    lhsT=identb[:, g : g + 1].to_broadcast([P, P]),
+                    rhs=bo16[:],
+                    start=True,
+                    stop=True,
+                )
+            nc.vector.tensor_copy(out=bo_bc[:, 1024 * c : 1024 * c + 1024], in_=bank[:])
+
+        def quantise(src, width, tag):
+            codes = cod.tile([P, width], U32, tag=tag + "c", name=tag + "c", align_bytes=64)
+            scales = cod.tile([P, width], U8, tag=tag + "s", name=tag + "s", align_bytes=64)
+            nc.vector.quantize_mx(out=codes[:].bitcast(FP8X4), scales=scales[:], in_=src[:])
+            return codes, scales
+
+        def mm1(g):
+            wc, ws = w3c[g]
+            ac, as_ = hc[g]
+            xs[g] = []
+            for half in range(2):
+                x = xp.tile([P, 512], F32, tag="x", name="x")
+                xs[g].append(x)
+                for i in range(2):
+                    t = 2 * half + i
+                    nc.tensor.matmul_mx(
+                        out=x[:, 256 * i : 256 * i + 256],
+                        lhsT=wc[:, 128 * t : 128 * t + 128].bitcast(FP8X4),
+                        lhsT_scale=ws[:, 128 * t : 128 * t + 128],
+                        rhs=ac[:].bitcast(FP8X4),
+                        rhs_scale=as_[:],
+                        start=True,
+                        stop=True,
+                    )
+
+        def relu(g):
+            r = res.tile([P, 4 * B], F32, tag="r", name="r")
+            rs[g] = r
+            for t in range(4):
+                nc.scalar.activation(
+                    out=r[:, 256 * t : 256 * t + 256],
+                    in_=xs[g][t // 2][:, 256 * (t % 2) : 256 * (t % 2) + 256],
+                    func=RELU,
+                    bias=b3c[:, 4 * g + t : 4 * g + t + 1],
+                    scale=1.0,
+                )
+
+        def residual(g):
+            s = grp.tile([P, 4 * B], BF16, tag="h3g", name="h3g", align_bytes=64)
+            h3g[g] = s
+            nc.vector.tensor_tensor(
+                out=s[:].rearrange("p (c i t) -> p c t i", i=4, t=4),
+                in0=rs[g][:].rearrange("p (t c i) -> p c t i", t=4, i=4),
+                in1=grouped[(g, "h")][:].rearrange("p (c i t) -> p c t i", i=4, t=4),
+                op=ADD,
+            )
+
+        def mm2(g):
+            ac, as_ = h3c[g]
+            wc, ws = woc[g]
+            ys[g] = []
+            for bb in range(2):
+                y = yp.tile([P, PD], F32, tag="y", name="y")
+                ys[g].append(y)
+                nc.tensor.matmul_mx(
+                    out=y[:],
+                    lhsT=ac[:, 128 * bb : 128 * bb + 128].bitcast(FP8X4),
+                    lhsT_scale=as_[:, 128 * bb : 128 * bb + 128],
+                    rhs=wc[:].bitcast(FP8X4),
+                    rhs_scale=ws[:],
+                    start=True,
+                    stop=True,
+                )
+
+        def add_bias(g):
+            if g % 2 == 0:
+                ots[g // 2] = res.tile([P, 2 * 2 * PD], F32, tag="ot", name="ot", bufs=3)
+            ot = ots[g // 2][:].rearrange("p (bb c) -> p bb c", bb=2)
+            c0 = PD * (g % 2)
+            for bb in range(2):
+                nc.vector.tensor_tensor(
+                    out=ot[:, bb, c0 : c0 + PD].rearrange("p (q r) -> p q r", r=4),
+                    in0=ys[g][bb][:].rearrange("p (r q) -> p q r", r=4),
+                    in1=bo_bc[:, PD * g : PD * g + PD].rearrange("p (q r) -> p q r", r=4),
+                    op=ADD,
+                )
+                if g == G - 1:
+                    nc.sync.dma_start(
+                        out=out_view[:, bb, PD * g : PD * g + PD], in_=ot[:, bb, c0 : c0 + PD]
+                    )
+
+        def store(g0, g1):
+            ot = ots[g0 // 2][:].rearrange("p (bb c) -> p bb c", bb=2)
+            c0 = PD * (g0 % 2)
+            nc.sync.dma_start(
+                out=out_view[:, :, PD * g0 : PD * g1], in_=ot[:, :, c0 : c0 + PD * (g1 - g0)]
+            )
+
+        for g in range(LOOKAHEAD):
+            load_w(g)
+        spread_bias(0)
+        flip(0, 0)
+        flip(0, 1)
+        bias3_to_partitions()
+        flip(0, 2)
+
+        for j in range(G + 2):
+            if j + LOOKAHEAD < G:
+                load_w(j + LOOKAHEAD)
+            g = j - 3
+            if 0 <= g < G - 2 and g % 2 == 1:
+                store(g - 1, g + 1)
+            if g == G - 2:
+                store(g, g + 1)
+            if 0 <= j - 2 < G - 1:
+                residual(j - 2)
+            if 0 <= j - 1 < G:
+                woc[j - 1] = quantise(grouped[(j - 1, "wo")], PD, "wo")
+            if 0 <= j - 2 < G - 1:
+                h3c[j - 2] = quantise(h3g[j - 2], B, "h3")
+            copy_out(j, 0)
+            copy_out(j, 1)
+            if j == 0:
+                flip(0, 3)
+            if 0 <= j - 1 < G:
+                mm1(j - 1)
+            copy_out(j, 2)
+            copy_out(j, 3)
+            flip(j, 4)
+            copy_out(j, 4)
+            if j < G:
+                w3c[j] = quantise(grouped[(j, "w3")], H, "w3")
+                hc[j] = quantise(grouped[(j, "h")], B, "h")
+            for c in HEAD_BIAS.get(j, ()):
+                spread_bias(c)
+            flip(j + 1, 0)
+            flip(j + 1, 1)
+            if 0 <= j - 1 < G:
+                relu(j - 1)
+            if 0 <= j - 2 < G:
+                mm2(j - 2)
+            if j - 1 == G - 1:
+                residual(G - 1)
+                h3c[G - 1] = quantise(h3g[G - 1], B, "h3")
+            if 0 <= j - 2 < G:
+                add_bias(j - 2)
+            flip(j + 1, 2)
+            flip(j + 1, 3)

@@ -206,11 +206,16 @@ def tile_linearwdecoder_pb_kernel(tc, h, W3, b3, Wo, bo, out):
                     stop=True,
                 )
 
+        def out_tile(g):
+            if g >= G - 2:
+                return g, 0
+            return g - g % 2, PD * (g % 2)
+
         def add_bias(g):
-            if g % 2 == 0:
-                ots[g // 2] = res.tile([P, 2 * 2 * PD], F32, tag="ot", name="ot", bufs=3)
-            ot = ots[g // 2][:].rearrange("p (bb c) -> p bb c", bb=2)
-            c0 = PD * (g % 2)
+            first, c0 = out_tile(g)
+            if first == g:
+                ots[g] = res.tile([P, 2 * 2 * PD], F32, tag="ot", name="ot", bufs=3)
+            ot = ots[first][:].rearrange("p (bb c) -> p bb c", bb=2)
             for bb in range(2):
                 nc.vector.tensor_tensor(
                     out=ot[:, bb, c0 : c0 + PD].rearrange("p (q r) -> p q r", r=4),
@@ -224,8 +229,8 @@ def tile_linearwdecoder_pb_kernel(tc, h, W3, b3, Wo, bo, out):
                     )
 
         def store(g0, g1):
-            ot = ots[g0 // 2][:].rearrange("p (bb c) -> p bb c", bb=2)
-            c0 = PD * (g0 % 2)
+            first, c0 = out_tile(g0)
+            ot = ots[first][:].rearrange("p (bb c) -> p bb c", bb=2)
             nc.sync.dma_start(
                 out=out_view[:, :, PD * g0 : PD * g1], in_=ot[:, :, c0 : c0 + PD * (g1 - g0)]
             )

@@ -15,10 +15,11 @@ P = 128
 B, G, H, PD = 256, 16, 512, 512
 FLOPS = 2 * B * G * H * (H + PD)
 
+VECTOR_HELPS = 2
+
 W_BUFS = 8
 LOOKAHEAD = W_BUFS - 1
-HEAD_BIAS = {0: (1, 2, 3), 1: (4, 5, 6), 2: (7,)}
-H_CHUNKS = ((0, 2), (2, 4), (4, 8), (8, 12), (12, 16))
+H_CHUNKS = ((0, 1), (1, 2), (2, 4), (4, 8), (8, 12), (12, 16))
 
 
 def tile_linearwdecoder_pb_kernel(tc, h, W3, b3, Wo, bo, out):
@@ -43,13 +44,10 @@ def tile_linearwdecoder_pb_kernel(tc, h, W3, b3, Wo, bo, out):
         bo16 = const.tile([P, PD], BF16)
         nc.vector.memset(b3n[:], 0.0)
         nc.vector.memset(bo16[:], 0.0)
-        nc.sync.dma_start(out=bo16[0:G, :], in_=bo)
-        nc.sync.dma_start(out=b3n[0:G, :], in_=b3)
         ident = const.tile([P, P], F32)
         make_identity(nc, ident[:])
-        identb = const.tile([P, P], BF16)
-        make_identity(nc, identb[:])
         b3c = const.tile([P, 4 * G], F32)
+        bo_words = const.tile([P, 2 * G], F32)
         bo_bc = const.tile([P, G * PD], BF16)
 
         h_words = {}
@@ -68,11 +66,16 @@ def tile_linearwdecoder_pb_kernel(tc, h, W3, b3, Wo, bo, out):
 
         def load_w(g):
             a = wnat.tile([P, 4 * H], BF16, tag="w3n", name="w3n")
-            nc.sync.dma_start(out=a[:], in_=w3_view[:, g])
+            for x in range(0, 4 * H, 2 * H) if g == 0 else (0,):
+                y = 2 * H + x if g == 0 else 4 * H
+                nc.sync.dma_start(out=a[:, x:y], in_=w3_view[:, g, x:y])
             w3n[g] = a
             for c in range(len(H_CHUNKS)):
                 if H_CHUNKS[c][0] == g:
                     load_h(c)
+            if g == 0:
+                nc.sync.dma_start(out=b3n[0:G, :], in_=b3)
+                nc.sync.dma_start(out=bo16[0:G, :], in_=bo)
             b = wnat.tile([P, 4 * H], BF16, tag="won", name="won")
             nc.sync.dma_start(out=b[:], in_=wo_view[:, g])
             won[g] = b
@@ -114,33 +117,39 @@ def tile_linearwdecoder_pb_kernel(tc, h, W3, b3, Wo, bo, out):
                 dst = grouped[(g, "h")][:].bitcast(F32)
             else:
                 dst = grouped[(g, "wo")][:].bitcast(F32)[:, 512 * (k - 3) : 512 * (k - 3) + 512]
-            nc.scalar.copy(
+            (nc.vector.tensor_copy if g < VECTOR_HELPS and k >= 3 else nc.scalar.copy)(
                 out=dst.rearrange("p (a q u) -> p a q u", a=2, u=2),
                 in_=banks[(g, k)][:].rearrange("p (a u q) -> p a q u", a=2, u=2),
             )
 
-        def bias3_to_partitions():
-            bank = tp.tile([P, 512], F32, tag="tp", name="b3bank")
-            words = b3n[:].bitcast(F32)
+        def biases_to_partitions():
+            bank = tp.tile([P, 512], F32, tag="tp", name="biasbank")
             for u in range(2):
-                nc.tensor.transpose(bank[:, 128 * u : 128 * u + 128], words[:, u:256:2], ident[:])
+                nc.tensor.transpose(bank[:, 128 * u : 128 * u + 128], b3n[:].bitcast(F32)[:, u:256:2], ident[:])
+            for h in range(2):
+                nc.tensor.transpose(
+                    bank[:, 256 + 128 * h : 384 + 128 * h], bo16[:].bitcast(F32)[:, 128 * h : 128 * h + 128], ident[:]
+                )
             nc.vector.tensor_copy(
                 out=b3c[:].rearrange("p (g u e) -> p u g e", u=2, e=2),
                 in_=bank[:, 0:256].bitcast(BF16).rearrange("p (u g e) -> p u g e", u=2, e=2)[:, :, 0:G, :],
             )
+            nc.vector.tensor_copy(
+                out=bo_words[:].rearrange("p (h g) -> p h g", h=2),
+                in_=bank[:, 256:512].rearrange("p (h g) -> p h g", h=2)[:, :, 0:G],
+            )
 
         def spread_bias(c):
-            bank = tp.tile([P, 1024], BF16, tag="tp", name="bbank")
+            bank = tp.tile([P, 512], F32, tag="tp", name="bbank")
             for i in range(2):
-                g = 2 * c + i
-                nc.tensor.matmul(
-                    bank[:, 512 * i : 512 * i + 512],
-                    lhsT=identb[:, g : g + 1].to_broadcast([P, P]),
-                    rhs=bo16[:],
-                    start=True,
-                    stop=True,
-                )
-            nc.vector.tensor_copy(out=bo_bc[:, 1024 * c : 1024 * c + 1024], in_=bank[:])
+                for h in range(2):
+                    w = G * h + 2 * c + i
+                    nc.tensor.transpose(
+                        bank[:, 256 * i + 128 * h : 256 * i + 128 * h + 128],
+                        bo_words[:, w : w + 1].to_broadcast([P, P]),
+                        ident[:],
+                    )
+            nc.scalar.copy(out=bo_bc[:].bitcast(F32)[:, 512 * c : 512 * c + 512], in_=bank[:])
 
         def quantise(src, width, tag):
             codes = cod.tile([P, width], U32, tag=tag + "c", name=tag + "c", align_bytes=64)
@@ -237,10 +246,8 @@ def tile_linearwdecoder_pb_kernel(tc, h, W3, b3, Wo, bo, out):
 
         for g in range(LOOKAHEAD):
             load_w(g)
-        spread_bias(0)
         flip(0, 0)
         flip(0, 1)
-        bias3_to_partitions()
         flip(0, 2)
 
         for j in range(G + 2):
@@ -264,14 +271,21 @@ def tile_linearwdecoder_pb_kernel(tc, h, W3, b3, Wo, bo, out):
             if 0 <= j - 1 < G:
                 mm1(j - 1)
             copy_out(j, 2)
-            copy_out(j, 3)
+            if j >= VECTOR_HELPS:
+                copy_out(j, 3)
             flip(j, 4)
-            copy_out(j, 4)
+            if j >= VECTOR_HELPS:
+                copy_out(j, 4)
             if j < G:
                 w3c[j] = quantise(grouped[(j, "w3")], H, "w3")
                 hc[j] = quantise(grouped[(j, "h")], B, "h")
-            for c in HEAD_BIAS.get(j, ()):
-                spread_bias(c)
+            if j < VECTOR_HELPS:
+                copy_out(j, 3)
+                copy_out(j, 4)
+            if j == 0:
+                biases_to_partitions()
+            if 0 < j < G and j % 2 == 1:
+                spread_bias(j // 2)
             flip(j + 1, 0)
             flip(j + 1, 1)
             if 0 <= j - 1 < G:

@@ -15,10 +15,9 @@ P = 128
 B, G, H, PD = 256, 16, 512, 512
 FLOPS = 2 * B * G * H * (H + PD)
 
-VECTOR_HELPS = 2
-
 W_BUFS = 8
 LOOKAHEAD = W_BUFS - 1
+SPREAD_SLOTS = (2, 4, 6, 8, 10, 12, 13, 14)
 H_CHUNKS = ((0, 1), (1, 2), (2, 4), (4, 8), (8, 12), (12, 16))
 
 
@@ -64,21 +63,23 @@ def tile_linearwdecoder_pb_kernel(tc, h, W3, b3, Wo, bo, out):
             for g in range(g0, g1):
                 h_words[g] = (t, [(bb * (g1 - g0) + g - g0) * 256 + u for bb in range(2) for u in range(2)])
 
-        def load_w(g):
-            a = wnat.tile([P, 4 * H], BF16, tag="w3n", name="w3n")
-            for x in range(0, 4 * H, 2 * H) if g == 0 else (0,):
-                y = 2 * H + x if g == 0 else 4 * H
-                nc.sync.dma_start(out=a[:, x:y], in_=w3_view[:, g, x:y])
-            w3n[g] = a
-            for c in range(len(H_CHUNKS)):
-                if H_CHUNKS[c][0] == g:
-                    load_h(c)
+        def load_code(g):
+            if g < G:
+                a = wnat.tile([P, 4 * H], BF16, tag="w3n", name="w3n")
+                width = 2 * H if g == 0 else 4 * H
+                for x in range(0, 4 * H, width):
+                    nc.sync.dma_start(out=a[:, x : x + width], in_=w3_view[:, g, x : x + width])
+                w3n[g] = a
+                for c in range(len(H_CHUNKS)):
+                    if H_CHUNKS[c][0] == g:
+                        load_h(c)
             if g == 0:
                 nc.sync.dma_start(out=b3n[0:G, :], in_=b3)
                 nc.sync.dma_start(out=bo16[0:G, :], in_=bo)
-            b = wnat.tile([P, 4 * H], BF16, tag="won", name="won")
-            nc.sync.dma_start(out=b[:], in_=wo_view[:, g])
-            won[g] = b
+            else:
+                b = wnat.tile([P, 4 * H], BF16, tag="won", name="won")
+                nc.sync.dma_start(out=b[:], in_=wo_view[:, g - 1])
+                won[g - 1] = b
 
         banks = {}
         grouped = {}
@@ -117,7 +118,7 @@ def tile_linearwdecoder_pb_kernel(tc, h, W3, b3, Wo, bo, out):
                 dst = grouped[(g, "h")][:].bitcast(F32)
             else:
                 dst = grouped[(g, "wo")][:].bitcast(F32)[:, 512 * (k - 3) : 512 * (k - 3) + 512]
-            (nc.vector.tensor_copy if g < VECTOR_HELPS and k >= 3 else nc.scalar.copy)(
+            nc.scalar.copy(
                 out=dst.rearrange("p (a q u) -> p a q u", a=2, u=2),
                 in_=banks[(g, k)][:].rearrange("p (a u q) -> p a q u", a=2, u=2),
             )
@@ -203,7 +204,7 @@ def tile_linearwdecoder_pb_kernel(tc, h, W3, b3, Wo, bo, out):
             wc, ws = woc[g]
             ys[g] = []
             for bb in range(2):
-                y = yp.tile([P, PD], F32, tag="y", name="y")
+                y = xp.tile([P, PD], F32, tag="x", name="x") if g == G - 1 else yp.tile([P, PD], F32, tag="y", name="y")
                 ys[g].append(y)
                 nc.tensor.matmul_mx(
                     out=y[:],
@@ -245,57 +246,39 @@ def tile_linearwdecoder_pb_kernel(tc, h, W3, b3, Wo, bo, out):
             )
 
         for g in range(LOOKAHEAD):
-            load_w(g)
-        flip(0, 0)
-        flip(0, 1)
-        flip(0, 2)
-
-        for j in range(G + 2):
-            if j + LOOKAHEAD < G:
-                load_w(j + LOOKAHEAD)
-            g = j - 3
-            if 0 <= g < G - 2 and g % 2 == 1:
-                store(g - 1, g + 1)
-            if g == G - 2:
-                store(g, g + 1)
-            if 0 <= j - 2 < G - 1:
-                residual(j - 2)
+            load_code(g)
+        for j in range(G + 3):
+            if j + LOOKAHEAD <= G:
+                load_code(j + LOOKAHEAD)
+            if 4 <= j < G + 2 and j % 2 == 1:
+                store(j - 5, j - 3)
             if 0 <= j - 1 < G:
-                woc[j - 1] = quantise(grouped[(j - 1, "wo")], PD, "wo")
-            if 0 <= j - 2 < G - 1:
+                hc[j - 1] = quantise(grouped[(j - 1, "h")], B, "h")
+            if 0 <= j - 2 < G:
+                residual(j - 2)
+                woc[j - 2] = quantise(grouped[(j - 2, "wo")], PD, "wo")
                 h3c[j - 2] = quantise(h3g[j - 2], B, "h3")
+            if 0 <= j - 3 < G:
+                mm2(j - 3)
+            flip(j, 0)
+            flip(j, 1)
             copy_out(j, 0)
             copy_out(j, 1)
-            if j == 0:
-                flip(0, 3)
             if 0 <= j - 1 < G:
                 mm1(j - 1)
+                relu(j - 1)
+            flip(j, 2)
             copy_out(j, 2)
-            if j >= VECTOR_HELPS:
-                copy_out(j, 3)
-            flip(j, 4)
-            if j >= VECTOR_HELPS:
-                copy_out(j, 4)
+            for k in (3, 4):
+                flip(j - 1, k)
+                copy_out(j - 1, k)
+            if 0 <= j - 3 < G:
+                add_bias(j - 3)
+            if j == G + 1:
+                store(G - 2, G - 1)
+            if j in SPREAD_SLOTS:
+                spread_bias(SPREAD_SLOTS.index(j))
             if j < G:
                 w3c[j] = quantise(grouped[(j, "w3")], H, "w3")
-                hc[j] = quantise(grouped[(j, "h")], B, "h")
-            if j < VECTOR_HELPS:
-                copy_out(j, 3)
-                copy_out(j, 4)
             if j == 0:
                 biases_to_partitions()
-            if 0 < j < G and j % 2 == 1:
-                spread_bias(j // 2)
-            flip(j + 1, 0)
-            flip(j + 1, 1)
-            if 0 <= j - 1 < G:
-                relu(j - 1)
-            if 0 <= j - 2 < G:
-                mm2(j - 2)
-            if j - 1 == G - 1:
-                residual(G - 1)
-                h3c[G - 1] = quantise(h3g[G - 1], B, "h3")
-            if 0 <= j - 2 < G:
-                add_bias(j - 2)
-            flip(j + 1, 2)
-            flip(j + 1, 3)

@@ -17,7 +17,7 @@ FLOPS = 2 * B * G * H * (H + PD)
 
 W_BUFS = 8
 LOOKAHEAD = W_BUFS - 1
-SPREAD_SLOTS = (2, 4, 6, 8, 10, 12, 13, 14)
+SPREAD_SLOTS = (2, 4)
 H_CHUNKS = ((0, 1), (1, 2), (2, 4), (4, 8), (8, 12), (12, 16))
 
 
@@ -37,6 +37,7 @@ def tile_linearwdecoder_pb_kernel(tc, h, W3, b3, Wo, bo, out):
         w3_view = W3.rearrange("g (q t) k -> q g (t k)", t=4)
         wo_view = Wo.rearrange("g (q r) k -> q g (r k)", r=4)
         h_view = h.rearrange("(bb m) g k -> m bb (g k)", m=P)
+        bo_flat = bo.rearrange("g c -> (g c)")
         out_view = out.rearrange("(bb m) c -> m bb c", m=P)
 
         b3n = const.tile([P, H], BF16)
@@ -80,6 +81,12 @@ def tile_linearwdecoder_pb_kernel(tc, h, W3, b3, Wo, bo, out):
                 b = wnat.tile([P, 4 * H], BF16, tag="won", name="won")
                 nc.sync.dma_start(out=b[:], in_=wo_view[:, g - 1])
                 won[g - 1] = b
+            c = g - 3
+            if len(SPREAD_SLOTS) <= c < G // 2:
+                nc.sync.dma_start(
+                    out=bo_bc[:, 2 * PD * c : 2 * PD * c + 2 * PD],
+                    in_=bo_flat[2 * PD * c : 2 * PD * c + 2 * PD].partition_broadcast(P),
+                )
 
         banks = {}
         grouped = {}
@@ -224,7 +231,7 @@ def tile_linearwdecoder_pb_kernel(tc, h, W3, b3, Wo, bo, out):
         def add_bias(g):
             first, c0 = out_tile(g)
             if first == g:
-                ots[g] = res.tile([P, 2 * 2 * PD], F32, tag="ot", name="ot", bufs=3)
+                ots[g] = res.tile([P, 2 * 2 * PD], F32, tag="ot", name="ot", bufs=5)
             ot = ots[first][:].rearrange("p (bb c) -> p bb c", bb=2)
             for bb in range(2):
                 nc.vector.tensor_tensor(

from contextlib import ExitStack

import concourse.mybir as mybir
from concourse.masks import make_identity

F32 = mybir.dt.float32
BF16 = mybir.dt.bfloat16
U32 = mybir.dt.uint32
U8 = mybir.dt.uint8
FP8X4 = mybir.dt.float8_e4m3fn_x4
ADD = mybir.AluOpType.add
RELU = mybir.ActivationFunctionType.Relu

P = 128
B, G, H, PD = 256, 16, 512, 512
FLOPS = 2 * B * G * H * (H + PD)

W_BUFS = 8
LOOKAHEAD = W_BUFS - 1
SPREAD_SLOTS = (2, 4)
H_CHUNKS = ((0, 1), (1, 2), (2, 4), (4, 8), (8, 12), (12, 16))


def tile_linearwdecoder_pb_kernel(tc, h, W3, b3, Wo, bo, out):
    nc = tc.nc
    with ExitStack() as ctx:
        const = ctx.enter_context(tc.tile_pool(name="const", bufs=1))
        wnat = ctx.enter_context(tc.tile_pool(name="wnat", bufs=W_BUFS))
        grp = ctx.enter_context(tc.tile_pool(name="grp", bufs=2))
        cod = ctx.enter_context(tc.tile_pool(name="cod", bufs=2))
        res = ctx.enter_context(tc.tile_pool(name="res", bufs=2))
        tp = ctx.enter_context(tc.psum_pool(name="tp", bufs=4))
        xp = ctx.enter_context(tc.psum_pool(name="xp", bufs=2))
        yp = ctx.enter_context(tc.psum_pool(name="yp", bufs=2))
        ctx.enter_context(tc.manual_schedule())

        w3_view = W3.rearrange("g (q t) k -> q g (t k)", t=4)
        wo_view = Wo.rearrange("g (q r) k -> q g (r k)", r=4)
        h_view = h.rearrange("(bb m) g k -> m bb (g k)", m=P)
        bo_flat = bo.rearrange("g c -> (g c)")
        out_view = out.rearrange("(bb m) c -> m bb c", m=P)

        b3n = const.tile([P, H], BF16)
        bo16 = const.tile([P, PD], BF16)
        nc.vector.memset(b3n[:], 0.0)
        nc.vector.memset(bo16[:], 0.0)
        ident = const.tile([P, P], F32)
        make_identity(nc, ident[:])
        b3c = const.tile([P, 4 * G], F32)
        bo_words = const.tile([P, 2 * G], F32)
        bo_bc = const.tile([P, G * PD], BF16)

        h_words = {}
        w3n = {}
        won = {}

        def load_h(c):
            g0, g1 = H_CHUNKS[c]
            t = const.tile([P, 2 * (g1 - g0) * H], BF16, name="hnat%d" % c)
            nc.sync.dma_start(
                out=t[:].rearrange("p (bb x) -> p bb x", bb=2),
                in_=h_view[:, :, g0 * H : g1 * H],
            )
            for g in range(g0, g1):
                h_words[g] = (t, [(bb * (g1 - g0) + g - g0) * 256 + u for bb in range(2) for u in range(2)])

        def load_code(g):
            if g < G:
                a = wnat.tile([P, 4 * H], BF16, tag="w3n", name="w3n")
                width = 2 * H if g == 0 else 4 * H
                for x in range(0, 4 * H, width):
                    nc.sync.dma_start(out=a[:, x : x + width], in_=w3_view[:, g, x : x + width])
                w3n[g] = a
                for c in range(len(H_CHUNKS)):
                    if H_CHUNKS[c][0] == g:
                        load_h(c)
            if g == 0:
                nc.sync.dma_start(out=b3n[0:G, :], in_=b3)
                nc.sync.dma_start(out=bo16[0:G, :], in_=bo)
            else:
                b = wnat.tile([P, 4 * H], BF16, tag="won", name="won")
                nc.sync.dma_start(out=b[:], in_=wo_view[:, g - 1])
                won[g - 1] = b
            c = g - 3
            if len(SPREAD_SLOTS) <= c < G // 2:
                nc.sync.dma_start(
                    out=bo_bc[:, 2 * PD * c : 2 * PD * c + 2 * PD],
                    in_=bo_flat[2 * PD * c : 2 * PD * c + 2 * PD].partition_broadcast(P),
                )

        banks = {}
        grouped = {}
        w3c, woc, hc, h3c = {}, {}, {}, {}
        h3g, xs, rs, ys, ots = {}, {}, {}, {}, {}

        def flip(g, k):
            if not 0 <= g < G:
                return
            if k < 2:
                src, offsets = w3n[g], [512 * k + 256 * a + u for a in range(2) for u in range(2)]
            elif k == 2:
                src, offsets = h_words[g]
            else:
                src, offsets = won[g], [512 * (k - 3) + 256 * a + u for a in range(2) for u in range(2)]
            bank = tp.tile([P, 512], F32, tag="tp", name="bank")
            banks[(g, k)] = bank
            words = src[:].bitcast(F32)
            for i in range(4):
                nc.tensor.transpose(
                    bank[:, 128 * i : 128 * i + 128], words[:, offsets[i] : offsets[i] + 255 : 2], ident[:]
                )

        def copy_out(g, k):
            if not 0 <= g < G:
                return
            if k == 0:
                grouped[(g, "w3")] = grp.tile([P, 4 * H], BF16, tag="w3g", name="w3g", align_bytes=64)
            if k == 2:
                grouped[(g, "h")] = grp.tile([P, 4 * B], BF16, tag="hg", name="hg", align_bytes=64, bufs=3)
            if k == 3:
                grouped[(g, "wo")] = grp.tile([P, 4 * PD], BF16, tag="wog", name="wog", align_bytes=64)
            if k < 2:
                dst = grouped[(g, "w3")][:].bitcast(F32)[:, 512 * k : 512 * k + 512]
            elif k == 2:
                dst = grouped[(g, "h")][:].bitcast(F32)
            else:
                dst = grouped[(g, "wo")][:].bitcast(F32)[:, 512 * (k - 3) : 512 * (k - 3) + 512]
            nc.scalar.copy(
                out=dst.rearrange("p (a q u) -> p a q u", a=2, u=2),
                in_=banks[(g, k)][:].rearrange("p (a u q) -> p a q u", a=2, u=2),
            )

        def biases_to_partitions():
            bank = tp.tile([P, 512], F32, tag="tp", name="biasbank")
            for u in range(2):
                nc.tensor.transpose(bank[:, 128 * u : 128 * u + 128], b3n[:].bitcast(F32)[:, u:256:2], ident[:])
            for h in range(2):
                nc.tensor.transpose(
                    bank[:, 256 + 128 * h : 384 + 128 * h], bo16[:].bitcast(F32)[:, 128 * h : 128 * h + 128], ident[:]
                )
            nc.vector.tensor_copy(
                out=b3c[:].rearrange("p (g u e) -> p u g e", u=2, e=2),
                in_=bank[:, 0:256].bitcast(BF16).rearrange("p (u g e) -> p u g e", u=2, e=2)[:, :, 0:G, :],
            )
            nc.vector.tensor_copy(
                out=bo_words[:].rearrange("p (h g) -> p h g", h=2),
                in_=bank[:, 256:512].rearrange("p (h g) -> p h g", h=2)[:, :, 0:G],
            )

        def spread_bias(c):
            bank = tp.tile([P, 512], F32, tag="tp", name="bbank")
            for i in range(2):
                for h in range(2):
                    w = G * h + 2 * c + i
                    nc.tensor.transpose(
                        bank[:, 256 * i + 128 * h : 256 * i + 128 * h + 128],
                        bo_words[:, w : w + 1].to_broadcast([P, P]),
                        ident[:],
                    )
            nc.scalar.copy(out=bo_bc[:].bitcast(F32)[:, 512 * c : 512 * c + 512], in_=bank[:])

        def quantise(src, width, tag):
            codes = cod.tile([P, width], U32, tag=tag + "c", name=tag + "c", align_bytes=64)
            scales = cod.tile([P, width], U8, tag=tag + "s", name=tag + "s", align_bytes=64)
            nc.vector.quantize_mx(out=codes[:].bitcast(FP8X4), scales=scales[:], in_=src[:])
            return codes, scales

        def mm1(g):
            wc, ws = w3c[g]
            ac, as_ = hc[g]
            xs[g] = []
            for half in range(2):
                x = xp.tile([P, 512], F32, tag="x", name="x")
                xs[g].append(x)
                for i in range(2):
                    t = 2 * half + i
                    nc.tensor.matmul_mx(
                        out=x[:, 256 * i : 256 * i + 256],
                        lhsT=wc[:, 128 * t : 128 * t + 128].bitcast(FP8X4),
                        lhsT_scale=ws[:, 128 * t : 128 * t + 128],
                        rhs=ac[:].bitcast(FP8X4),
                        rhs_scale=as_[:],
                        start=True,
                        stop=True,
                    )

        def relu(g):
            r = res.tile([P, 4 * B], F32, tag="r", name="r")
            rs[g] = r
            for t in range(4):
                nc.scalar.activation(
                    out=r[:, 256 * t : 256 * t + 256],
                    in_=xs[g][t // 2][:, 256 * (t % 2) : 256 * (t % 2) + 256],
                    func=RELU,
                    bias=b3c[:, 4 * g + t : 4 * g + t + 1],
                    scale=1.0,
                )

        def residual(g):
            s = grp.tile([P, 4 * B], BF16, tag="h3g", name="h3g", align_bytes=64)
            h3g[g] = s
            nc.vector.tensor_tensor(
                out=s[:].rearrange("p (c i t) -> p c t i", i=4, t=4),
                in0=rs[g][:].rearrange("p (t c i) -> p c t i", t=4, i=4),
                in1=grouped[(g, "h")][:].rearrange("p (c i t) -> p c t i", i=4, t=4),
                op=ADD,
            )

        def mm2(g):
            ac, as_ = h3c[g]
            wc, ws = woc[g]
            ys[g] = []
            for bb in range(2):
                y = xp.tile([P, PD], F32, tag="x", name="x") if g == G - 1 else yp.tile([P, PD], F32, tag="y", name="y")
                ys[g].append(y)
                nc.tensor.matmul_mx(
                    out=y[:],
                    lhsT=ac[:, 128 * bb : 128 * bb + 128].bitcast(FP8X4),
                    lhsT_scale=as_[:, 128 * bb : 128 * bb + 128],
                    rhs=wc[:].bitcast(FP8X4),
                    rhs_scale=ws[:],
                    start=True,
                    stop=True,
                )

        def out_tile(g):
            if g >= G - 2:
                return g, 0
            return g - g % 2, PD * (g % 2)

        def add_bias(g):
            first, c0 = out_tile(g)
            if first == g:
                ots[g] = res.tile([P, 2 * 2 * PD], F32, tag="ot", name="ot", bufs=5)
            ot = ots[first][:].rearrange("p (bb c) -> p bb c", bb=2)
            for bb in range(2):
                nc.vector.tensor_tensor(
                    out=ot[:, bb, c0 : c0 + PD].rearrange("p (q r) -> p q r", r=4),
                    in0=ys[g][bb][:].rearrange("p (r q) -> p q r", r=4),
                    in1=bo_bc[:, PD * g : PD * g + PD].rearrange("p (q r) -> p q r", r=4),
                    op=ADD,
                )
                if g == G - 1:
                    nc.sync.dma_start(
                        out=out_view[:, bb, PD * g : PD * g + PD], in_=ot[:, bb, c0 : c0 + PD]
                    )

        def store(g0, g1):
            first, c0 = out_tile(g0)
            ot = ots[first][:].rearrange("p (bb c) -> p bb c", bb=2)
            nc.sync.dma_start(
                out=out_view[:, :, PD * g0 : PD * g1], in_=ot[:, :, c0 : c0 + PD * (g1 - g0)]
            )

        for g in range(LOOKAHEAD):
            load_code(g)
        for j in range(G + 3):
            if j + LOOKAHEAD <= G:
                load_code(j + LOOKAHEAD)
            if 4 <= j < G + 2 and j % 2 == 1:
                store(j - 5, j - 3)
            if 0 <= j - 1 < G:
                hc[j - 1] = quantise(grouped[(j - 1, "h")], B, "h")
            if 0 <= j - 2 < G:
                residual(j - 2)
                woc[j - 2] = quantise(grouped[(j - 2, "wo")], PD, "wo")
                h3c[j - 2] = quantise(h3g[j - 2], B, "h3")
            if 0 <= j - 3 < G:
                mm2(j - 3)
            flip(j, 0)
            flip(j, 1)
            copy_out(j, 0)
            copy_out(j, 1)
            if 0 <= j - 1 < G:
                mm1(j - 1)
                relu(j - 1)
            flip(j, 2)
            copy_out(j, 2)
            for k in (3, 4):
                flip(j - 1, k)
                copy_out(j - 1, k)
            if 0 <= j - 3 < G:
                add_bias(j - 3)
            if j == G + 1:
                store(G - 2, G - 1)
            if j in SPREAD_SLOTS:
                spread_bias(SPREAD_SLOTS.index(j))
            if j < G:
                w3c[j] = quantise(grouped[(j, "w3")], H, "w3")
            if j == 0:
                biases_to_partitions()
